import numpy as np
import ml_dtypes


def mxq(x, axis, fmt="e4m3"):
    dtype, down = {"e4m3": (ml_dtypes.float8_e4m3fn, 7), "e5m2": (ml_dtypes.float8_e5m2, 14)}[fmt]
    v = np.moveaxis(np.asarray(x, np.float32).astype(ml_dtypes.bfloat16).astype(np.float64), axis, -1)
    blocks = v.reshape(v.shape[:-1] + (-1, 32))
    amax = np.abs(blocks).max(-1, keepdims=True)
    byte = np.maximum(np.where(amax > 0, np.frexp(amax)[1] - 1 + 127, 0) - down, 1)
    scale = np.exp2(byte - 127.0)
    codes = (blocks / scale).astype(np.float32).astype(dtype).astype(np.float64)
    return np.moveaxis((codes * scale).reshape(v.shape), -1, axis)


WIDE = False


def mx_kscale(k):
    if not WIDE:
        return np.ones(k)
    levels = np.array([10, -10, 5, -5, 0])
    a = np.random.permutation(np.resize(levels, k // 512 * 4)).reshape(k // 512, 4)
    idx = np.arange(k)
    return np.exp2(a[idx // 512, idx % 128 // 32])


BF16 = ml_dtypes.bfloat16


def bf(x):
    return np.asarray(x, np.float32).astype(BF16)


def f64(x):
    return np.asarray(x).astype(np.float64)


E2M1 = np.array([0.0, 0.5, 1.0, 1.5, 2.0, 3.0, 4.0, 6.0, -0.0, -0.5, -1.0, -1.5, -2.0, -3.0, -4.0, -6.0])


def pack_weight(w, fmt):
    k, n = w.shape
    w = f64(bf(w)).reshape(k // 32, 32, n)
    amax = np.abs(w).max(1)
    if fmt == "e4m3":
        byte = np.frexp(amax)[1] - 1 + 127 - 7
    else:
        mant, ex = np.frexp(amax / 6.0)
        byte = np.where(mant > 0.5, ex, ex - 1) + 127
    byte = np.clip(np.where(amax > 0, byte, 1), 1, 254)
    scaled = (w * np.exp2(127.0 - byte)[:, None, :]).reshape(k, n).astype(np.float32)
    by_word = np.ascontiguousarray(scaled.reshape(k // 512, 128, 4, n).transpose(0, 1, 3, 2))
    if fmt == "e4m3":
        words = by_word.astype(ml_dtypes.float8_e4m3fn).view(np.uint8)
    else:
        c = by_word.astype(ml_dtypes.float4_e2m1fn).view(np.uint8) & 0xF
        words = c[..., 0::2] | (c[..., 1::2] << 4)
    return np.ascontiguousarray(words), np.ascontiguousarray(byte.astype(np.uint8).reshape(k // 512, 16, n))


def unpack_weight(words, scales, fmt):
    g, p, n, _ = words.shape
    if fmt == "e4m3":
        vals = np.ascontiguousarray(words).view(ml_dtypes.float8_e4m3fn).astype(np.float64)
    else:
        nib = np.empty((g, p, n, 4), np.uint8)
        nib[..., 0::2] = words & 0xF
        nib[..., 1::2] = words >> 4
        vals = E2M1[nib]
    vals = vals * np.repeat(np.exp2(scales.astype(np.float64) - 127.0), 8, axis=1)[..., None]
    return vals.transpose(0, 1, 3, 2).reshape(g * 512, n)


B, P0, P1, P2, K0, K1, K2 = 128, 4096, 9216, 7168, 512, 512, 512
PT = P0 + P1 + P2
KT = K0 + K1 + K2
CLIP0 = 1.0
FMT = "e4m3"


def clip_rows(mat, clip):
    norms = np.sqrt(np.sum(mat * mat, axis=1, keepdims=True))
    scale = np.minimum(clip / norms, 1.0)
    return mat * scale


def setup_inputs():
    s0, s1, s2 = mx_kscale(P0), mx_kscale(P1), mx_kscale(P2)
    r = np.exp2(np.random.uniform(-2.0, 2.0, (B, 1))) / (KT * PT) ** 0.25
    target_grad = bf(np.random.standard_normal((B, PT)) * r * np.concatenate([s0, s1, s2]))
    words0, scales0 = pack_weight(np.random.standard_normal((P0, K0)) / np.sqrt(P0) / s0[:, None], FMT)
    words1, scales1 = pack_weight(np.random.standard_normal((P1, K1)) / np.sqrt(P1) / s1[:, None], FMT)
    words2, scales2 = pack_weight(np.random.standard_normal((P2, K2)) / np.sqrt(P2) / s2[:, None], FMT)
    return {"target_grad": target_grad,
            "bases0_words": words0, "bases0_scales": scales0,
            "bases1_words": words1, "bases1_scales": scales1,
            "bases2_words": words2, "bases2_scales": scales2}


def reference(target_grad, bases0_words, bases0_scales, bases1_words, bases1_scales, bases2_words, bases2_scales):
    g = f64(target_grad)
    embeddings = []
    offset = 0
    for b in (unpack_weight(bases0_words, bases0_scales, FMT),
              unpack_weight(bases1_words, bases1_scales, FMT),
              unpack_weight(bases2_words, bases2_scales, FMT)):
        num_p = b.shape[0]
        embeddings.append(mxq(g[:, offset:offset + num_p], 1, "e4m3") @ b)
        offset += num_p
    embedding = np.concatenate(embeddings, axis=1)
    avg_clipped_embedding = np.sum(clip_rows(embedding, CLIP0), axis=0) / B
    return embedding, avg_clipped_embedding

@@ -1,0 +1,195 @@
+from contextlib import ExitStack
+
+import concourse.mybir as mybir
+from concourse.masks import make_identity
+
+F32 = mybir.dt.float32
+BF16 = mybir.dt.bfloat16
+I32 = mybir.dt.int32
+U32 = mybir.dt.uint32
+U8 = mybir.dt.uint8
+FP8X4 = mybir.dt.float8_e4m3fn_x4
+ACT = mybir.ActivationFunctionType
+ALU = mybir.AluOpType
+
+P = 128
+PACK = 4
+K_PASS = P * PACK
+N = 512
+PASSES = (8, 18, 14)
+FIRST_PASS = (0, 8, 26)
+ALL_PASSES = 40
+
+X_CHUNK = 8
+QUAD = 4
+PAIR = 2
+QUADRANTS = 4
+SCALE_DMAS_PER_LOAD = 3
+
+FLOPS = 2 * P * ALL_PASSES * K_PASS * N
+
+
+def tile_gep_pa_kernel(
+    tc,
+    target_grad,
+    bases0_words,
+    bases0_scales,
+    bases1_words,
+    bases1_scales,
+    bases2_words,
+    bases2_scales,
+    out_0,
+    out_1,
+):
+    nc = tc.nc
+    words = (bases0_words, bases1_words, bases2_words)
+    scales = (bases0_scales, bases1_scales, bases2_scales)
+
+    with ExitStack() as ctx:
+        ctx.enter_context(tc.manual_schedule())
+        keep = ctx.enter_context(tc.tile_pool(name="keep", bufs=1))
+        stage = ctx.enter_context(tc.tile_pool(name="stage", bufs=3))
+        psum_t = ctx.enter_context(tc.psum_pool(name="psum_t", bufs=4))
+        psum_e = ctx.enter_context(tc.psum_pool(name="psum_e", bufs=1))
+
+        slots = []
+        for b in range(3):
+            for g0 in range(0, PASSES[b], QUAD):
+                slots.append((b, g0, min(QUAD, PASSES[b] - g0)))
+
+        planes = keep.tile([P, len(slots) * N], U8, align_bytes=64)
+        nc.vector.memset(planes[:].bitcast(I32), 0)
+        one = keep.tile([P, 1], F32)
+        nc.vector.memset(one[:], 1.0)
+        warm = keep.tile([P, 1], F32)
+        nc.scalar.activation(out=warm[:], in_=one[:], func=ACT.Sqrt)
+        ident = keep.tile([P, P], F32)
+        make_identity(nc, ident[:])
+
+        scale_jobs = [(s, q) for s in range(len(slots)) for q in range(QUADRANTS)]
+
+        def load_scales(jobs):
+            for s, q in jobs:
+                b, g0, n = slots[s]
+                nc.sync.dma_start(
+                    out=planes[32 * q : 32 * q + 4 * n, s * N : (s + 1) * N].bitcast(I32),
+                    in_=scales[b][g0 : g0 + n, 4 * q : 4 * q + 4, :].bitcast(I32),
+                )
+
+        loads = 0
+        x_sb = []
+        for c in range(ALL_PASSES // X_CHUNK):
+            x_c = keep.tile([P, X_CHUNK * K_PASS], BF16, name="x%d" % c)
+            nc.sync.dma_start(
+                out=x_c[:], in_=target_grad[:, c * X_CHUNK * K_PASS : (c + 1) * X_CHUNK * K_PASS]
+            )
+            x_sb.append(x_c)
+            load_scales(scale_jobs[loads * SCALE_DMAS_PER_LOAD : (loads + 1) * SCALE_DMAS_PER_LOAD])
+            loads += 1
+        w_sb = []
+        for s in range(len(slots)):
+            b, g0, n = slots[s]
+            w_s = keep.tile([P, n, N], U32, name="w%d" % s, align_bytes=64)
+            nc.sync.dma_start(
+                out=w_s[:].bitcast(I32),
+                in_=words[b][g0 : g0 + n].rearrange("g p n t -> p g (n t)").bitcast(I32),
+            )
+            w_sb.append(w_s)
+            load_scales(scale_jobs[loads * SCALE_DMAS_PER_LOAD : (loads + 1) * SCALE_DMAS_PER_LOAD])
+            loads += 1
+        assert loads * SCALE_DMAS_PER_LOAD >= len(scale_jobs)
+
+        x_codes = keep.tile([P, ALL_PASSES * P], U32, align_bytes=64)
+        x_planes = keep.tile([P, ALL_PASSES * P], U8, align_bytes=64)
+
+        def quantise(first_pass, grouped):
+            cols = slice(first_pass * P, (first_pass + QUAD) * P)
+            nc.vector.quantize_mx(
+                out=x_codes[:, cols].bitcast(FP8X4), scales=x_planes[:, cols], in_=grouped[:]
+            )
+
+        waiting = None
+        for g0 in range(0, ALL_PASSES, QUAD):
+            grouped = stage.tile([P, QUAD * P * PACK], BF16, align_bytes=64)
+            grouped_words = grouped[:].bitcast(F32).rearrange(
+                "p (g b u) -> p g b u", g=QUAD, b=P
+            )
+            for h in range(QUAD // PAIR):
+                xt = psum_t.tile([P, PAIR, 2, P], F32)
+                for j in range(PAIR):
+                    g = g0 + h * PAIR + j
+                    x_words = x_sb[g // X_CHUNK][:].bitcast(F32)
+                    w0 = (g % X_CHUNK) * (K_PASS // 2)
+                    for u in range(2):
+                        nc.tensor.transpose(
+                            xt[:, j, u, :], x_words[:, w0 + u : w0 + K_PASS // 2 : 2], ident[:]
+                        )
+                copy = nc.vector.tensor_copy if h % 2 == 0 else nc.scalar.copy
+                copy(
+                    out=grouped_words[:, h * PAIR : (h + 1) * PAIR],
+                    in_=xt[:].rearrange("p g u b -> p g b u"),
+                )
+            if waiting is not None:
+                quantise(*waiting)
+            waiting = (g0, grouped)
+        quantise(*waiting)
+
+        e_sb = keep.tile([P, 3, N], F32)
+        squares = keep.tile([P, 3, N], F32)
+        sumsq = keep.tile([P, 3], F32)
+
+        def keep_embedding(b, acc):
+            nc.vector.tensor_copy(out=e_sb[:, b, :], in_=acc[:])
+            nc.sync.dma_start(out=out_0[:, b * N : (b + 1) * N], in_=e_sb[:, b, :])
+
+        accs = []
+        for b in range(3):
+            acc = psum_e.tile([P, N], F32, name="acc%d" % b)
+            accs.append(acc)
+        for s in range(len(slots)):
+            b, g0, n = slots[s]
+            for i in range(n):
+                g = FIRST_PASS[b] + g0 + i
+                nc.tensor.matmul_mx(
+                    out=accs[b][:],
+                    lhsT=x_codes[:, g * P : (g + 1) * P].bitcast(FP8X4),
+                    lhsT_scale=x_planes[:, g * P : (g + 1) * P],
+                    rhs=w_sb[s][:, i, :].bitcast(FP8X4),
+                    rhs_scale=planes[4 * i : P, s * N : (s + 1) * N],
+                    start=(g0 + i == 0),
+                    stop=(g0 + i == PASSES[b] - 1),
+                )
+            if g0 + n == PASSES[b]:
+                nc.scalar.activation(
+                    out=squares[:, b, :], in_=accs[b][:], func=ACT.Square,
+                    accum_out=sumsq[:, b : b + 1],
+                )
+                if b < 2:
+                    keep_embedding(b, accs[b])
+
+        early = keep.tile([P, 1], F32)
+        nc.vector.tensor_add(out=early[:], in0=sumsq[:, 0:1], in1=sumsq[:, 1:2])
+        clipped = keep.tile([P, 1], F32)
+        nc.vector.tensor_scalar(
+            out=clipped[:], in0=sumsq[:, 2:3], scalar1=early[:], scalar2=1.0,
+            op0=ALU.add, op1=ALU.max,
+        )
+        norm = keep.tile([P, 1], F32)
+        nc.scalar.activation(out=norm[:], in_=clipped[:], func=ACT.Sqrt, scale=float(P * P))
+        factor = keep.tile([P, 1], F32)
+        nc.vector.reciprocal(out=factor[:], in_=norm[:])
+        keep_embedding(2, accs[2])
+
+        avg_sb = keep.tile([P, 3, N], F32)
+        for b in range(3):
+            avg = psum_t.tile([P, N], F32, tag="xt")
+            nc.tensor.matmul(
+                out=avg[:], lhsT=factor[:, 0:1].to_broadcast([P, P]), rhs=e_sb[:, b, :],
+                start=True, stop=True,
+            )
+            copy = nc.vector.tensor_copy if b % 2 == 0 else nc.scalar.copy
+            copy(out=avg_sb[0:1, b, :], in_=avg[0:1, :])
+        nc.sync.dma_start(
+            out=out_1.rearrange("(o n) -> o n", o=1),
+            in_=avg_sb[0:1].rearrange("o b n -> o (b n)"),
+        )

@@ -24,7 +24,8 @@ X_CHUNK = 8
 QUAD = 4
 PAIR = 2
 QUADRANTS = 4
-SCALE_DMAS_PER_LOAD = 3
+LANES = ((0, 0, 8), (1, 0, 9), (1, 9, 9), (2, 0, 14))
+LANE_WIDTH = 14
 
 FLOPS = 2 * P * ALL_PASSES * K_PASS * N
 
@@ -57,7 +58,7 @@ def tile_gep_pa_kernel(
             for g0 in range(0, PASSES[b], QUAD):
                 slots.append((b, g0, min(QUAD, PASSES[b] - g0)))
 
-        planes = keep.tile([P, len(slots) * N], U8, align_bytes=64)
+        planes = keep.tile([P, LANE_WIDTH * N], U8, align_bytes=64)
         nc.vector.memset(planes[:].bitcast(I32), 0)
         one = keep.tile([P, 1], F32)
         nc.vector.memset(one[:], 1.0)
@@ -66,17 +67,26 @@ def tile_gep_pa_kernel(
         ident = keep.tile([P, P], F32)
         make_identity(nc, ident[:])
 
-        scale_jobs = [(s, q) for s in range(len(slots)) for q in range(QUADRANTS)]
-
-        def load_scales(jobs):
-            for s, q in jobs:
-                b, g0, n = slots[s]
-                nc.sync.dma_start(
-                    out=planes[32 * q : 32 * q + 4 * n, s * N : (s + 1) * N].bitcast(I32),
-                    in_=scales[b][g0 : g0 + n, 4 * q : 4 * q + 4, :].bitcast(I32),
+        for lane in range(len(LANES)):
+            b, g0, n = LANES[lane]
+            for q in range(QUADRANTS):
+                first = 32 * q + 4 * lane
+                nc.gpsimd.dma_start(
+                    out=planes[first : first + 4, 0 : n * N]
+                    .bitcast(F32)
+                    .rearrange("r (g n) -> r g n", g=n),
+                    in_=scales[b][g0 : g0 + n, 4 * q : 4 * q + 4, :]
+                    .rearrange("g r n -> r g n")
+                    .bitcast(F32),
                 )
 
-        loads = 0
+        def plane_of(b, g):
+            for lane in range(len(LANES)):
+                basis, g0, n = LANES[lane]
+                if basis == b and g0 <= g < g0 + n:
+                    return lane, g - g0
+            raise ValueError("no such pass")
+
         x_sb = []
         for c in range(ALL_PASSES // X_CHUNK):
             x_c = keep.tile([P, X_CHUNK * K_PASS], BF16, name="x%d" % c)
@@ -84,8 +94,6 @@ def tile_gep_pa_kernel(
                 out=x_c[:], in_=target_grad[:, c * X_CHUNK * K_PASS : (c + 1) * X_CHUNK * K_PASS]
             )
             x_sb.append(x_c)
-            load_scales(scale_jobs[loads * SCALE_DMAS_PER_LOAD : (loads + 1) * SCALE_DMAS_PER_LOAD])
-            loads += 1
         w_sb = []
         for s in range(len(slots)):
             b, g0, n = slots[s]
@@ -95,9 +103,6 @@ def tile_gep_pa_kernel(
                 in_=words[b][g0 : g0 + n].rearrange("g p n t -> p g (n t)").bitcast(I32),
             )
             w_sb.append(w_s)
-            load_scales(scale_jobs[loads * SCALE_DMAS_PER_LOAD : (loads + 1) * SCALE_DMAS_PER_LOAD])
-            loads += 1
-        assert loads * SCALE_DMAS_PER_LOAD >= len(scale_jobs)
 
         x_codes = keep.tile([P, ALL_PASSES * P], U32, align_bytes=64)
         x_planes = keep.tile([P, ALL_PASSES * P], U8, align_bytes=64)
@@ -150,12 +155,13 @@ def tile_gep_pa_kernel(
             b, g0, n = slots[s]
             for i in range(n):
                 g = FIRST_PASS[b] + g0 + i
+                lane, place = plane_of(b, g0 + i)
                 nc.tensor.matmul_mx(
                     out=accs[b][:],
                     lhsT=x_codes[:, g * P : (g + 1) * P].bitcast(FP8X4),
                     lhsT_scale=x_planes[:, g * P : (g + 1) * P],
                     rhs=w_sb[s][:, i, :].bitcast(FP8X4),
-                    rhs_scale=planes[4 * i : P, s * N : (s + 1) * N],
+                    rhs_scale=planes[4 * lane : P, place * N : (place + 1) * N],
                     start=(g0 + i == 0),
                     stop=(g0 + i == PASSES[b] - 1),
                 )

@@ -24,8 +24,7 @@ X_CHUNK = 8
 QUAD = 4
 PAIR = 2
 QUADRANTS = 4
-LANES = ((0, 0, 8), (1, 0, 9), (1, 9, 9), (2, 0, 14))
-LANE_WIDTH = 14
+SCALE_DMAS_PER_LOAD = 3
 
 FLOPS = 2 * P * ALL_PASSES * K_PASS * N
 
@@ -58,7 +57,7 @@ def tile_gep_pa_kernel(
             for g0 in range(0, PASSES[b], QUAD):
                 slots.append((b, g0, min(QUAD, PASSES[b] - g0)))
 
-        planes = keep.tile([P, LANE_WIDTH * N], U8, align_bytes=64)
+        planes = keep.tile([P, len(slots) * N], U8, align_bytes=64)
         nc.vector.memset(planes[:].bitcast(I32), 0)
         one = keep.tile([P, 1], F32)
         nc.vector.memset(one[:], 1.0)
@@ -67,26 +66,19 @@ def tile_gep_pa_kernel(
         ident = keep.tile([P, P], F32)
         make_identity(nc, ident[:])
 
-        for lane in range(len(LANES)):
-            b, g0, n = LANES[lane]
-            for q in range(QUADRANTS):
-                first = 32 * q + 4 * lane
-                nc.gpsimd.dma_start(
-                    out=planes[first : first + 4, 0 : n * N]
-                    .bitcast(F32)
-                    .rearrange("r (g n) -> r g n", g=n),
-                    in_=scales[b][g0 : g0 + n, 4 * q : 4 * q + 4, :]
-                    .rearrange("g r n -> r g n")
-                    .bitcast(F32),
+        def load_scales(queue, view, jobs):
+            for s, q in jobs:
+                b, g0, n = slots[s]
+                queue.dma_start(
+                    out=planes[32 * q : 32 * q + 4 * n, s * N : (s + 1) * N].bitcast(view),
+                    in_=scales[b][g0 : g0 + n, 4 * q : 4 * q + 4, :].bitcast(view),
                 )
 
-        def plane_of(b, g):
-            for lane in range(len(LANES)):
-                basis, g0, n = LANES[lane]
-                if basis == b and g0 <= g < g0 + n:
-                    return lane, g - g0
-            raise ValueError("no such pass")
+        all_jobs = [(s, q) for s in range(len(slots)) for q in range(QUADRANTS)]
+        load_scales(nc.gpsimd, F32, [(s, q) for s, q in all_jobs if slots[s][0] == 2])
+        scale_jobs = [(s, q) for s, q in all_jobs if slots[s][0] < 2]
 
+        loads = 0
         x_sb = []
         for c in range(ALL_PASSES // X_CHUNK):
             x_c = keep.tile([P, X_CHUNK * K_PASS], BF16, name="x%d" % c)
@@ -94,6 +86,11 @@ def tile_gep_pa_kernel(
                 out=x_c[:], in_=target_grad[:, c * X_CHUNK * K_PASS : (c + 1) * X_CHUNK * K_PASS]
             )
             x_sb.append(x_c)
+            load_scales(
+                nc.sync, I32,
+                scale_jobs[loads * SCALE_DMAS_PER_LOAD : (loads + 1) * SCALE_DMAS_PER_LOAD],
+            )
+            loads += 1
         w_sb = []
         for s in range(len(slots)):
             b, g0, n = slots[s]
@@ -103,6 +100,12 @@ def tile_gep_pa_kernel(
                 in_=words[b][g0 : g0 + n].rearrange("g p n t -> p g (n t)").bitcast(I32),
             )
             w_sb.append(w_s)
+            load_scales(
+                nc.sync, I32,
+                scale_jobs[loads * SCALE_DMAS_PER_LOAD : (loads + 1) * SCALE_DMAS_PER_LOAD],
+            )
+            loads += 1
+        assert loads * SCALE_DMAS_PER_LOAD >= len(scale_jobs)
 
         x_codes = keep.tile([P, ALL_PASSES * P], U32, align_bytes=64)
         x_planes = keep.tile([P, ALL_PASSES * P], U8, align_bytes=64)
@@ -155,13 +158,12 @@ def tile_gep_pa_kernel(
             b, g0, n = slots[s]
             for i in range(n):
                 g = FIRST_PASS[b] + g0 + i
-                lane, place = plane_of(b, g0 + i)
                 nc.tensor.matmul_mx(
                     out=accs[b][:],
                     lhsT=x_codes[:, g * P : (g + 1) * P].bitcast(FP8X4),
                     lhsT_scale=x_planes[:, g * P : (g + 1) * P],
                     rhs=w_sb[s][:, i, :].bitcast(FP8X4),
-                    rhs_scale=planes[4 * lane : P, place * N : (place + 1) * N],
+                    rhs_scale=planes[4 * i : P, s * N : (s + 1) * N],
                     start=(g0 + i == 0),
                     stop=(g0 + i == PASSES[b] - 1),
                 )

@@ -25,6 +25,7 @@ QUAD = 4
 PAIR = 2
 QUADRANTS = 4
 SCALE_DMAS_PER_LOAD = 3
+FILLERS = 6
 
 FLOPS = 2 * P * ALL_PASSES * K_PASS * N
 
@@ -51,6 +52,7 @@ def tile_gep_pa_kernel(
         stage = ctx.enter_context(tc.tile_pool(name="stage", bufs=3))
         psum_t = ctx.enter_context(tc.psum_pool(name="psum_t", bufs=4))
         psum_e = ctx.enter_context(tc.psum_pool(name="psum_e", bufs=1))
+        psum_d = ctx.enter_context(tc.psum_pool(name="psum_d", bufs=1))
 
         slots = []
         for b in range(3):
@@ -174,6 +176,10 @@ def tile_gep_pa_kernel(
                 )
                 if b < 2:
                     keep_embedding(b, accs[b])
+
+        filler = psum_d.tile([P, P], F32)
+        for i in range(FILLERS):
+            nc.tensor.matmul(out=filler[:], lhsT=ident[:], rhs=ident[:], start=True, stop=True)
 
         early = keep.tile([P, 1], F32)
         nc.vector.tensor_add(out=early[:], in0=sumsq[:, 0:1], in1=sumsq[:, 1:2])

@@ -64,7 +64,7 @@ def tile_gep_pa_kernel(
         one = keep.tile([P, 1], F32)
         nc.vector.memset(one[:], 1.0)
         warm = keep.tile([P, 1], F32)
-        nc.scalar.activation(out=warm[:], in_=one[:], func=ACT.Sqrt)
+        nc.scalar.activation(out=warm[:], in_=one[:], func=ACT.Abs_reciprocal_sqrt)
         ident = keep.tile([P, P], F32)
         make_identity(nc, ident[:])
 
@@ -183,27 +183,25 @@ def tile_gep_pa_kernel(
 
         early = keep.tile([P, 1], F32)
         nc.vector.tensor_add(out=early[:], in0=sumsq[:, 0:1], in1=sumsq[:, 1:2])
-        clipped = keep.tile([P, 1], F32)
-        nc.vector.tensor_scalar(
-            out=clipped[:], in0=sumsq[:, 2:3], scalar1=early[:], scalar2=1.0,
-            op0=ALU.add, op1=ALU.max,
+        inverse = keep.tile([P, 1], F32)
+        nc.scalar.activation(
+            out=inverse[:], in_=sumsq[:, 2:3], func=ACT.Abs_reciprocal_sqrt, bias=early[:]
         )
-        norm = keep.tile([P, 1], F32)
-        nc.scalar.activation(out=norm[:], in_=clipped[:], func=ACT.Sqrt, scale=float(P * P))
         factor = keep.tile([P, 1], F32)
-        nc.vector.reciprocal(out=factor[:], in_=norm[:])
+        nc.vector.tensor_scalar(
+            out=factor[:], in0=inverse[:], scalar1=1.0, scalar2=1.0 / P, op0=ALU.min, op1=ALU.mult
+        )
         keep_embedding(2, accs[2])
 
-        avg_sb = keep.tile([P, 3, N], F32)
-        for b in range(3):
+        avg_sb = keep.tile([P, 3 * N], F32)
+        e_flat = e_sb[:].rearrange("p b n -> p (b n)")
+        pieces = [(0, N), (N, N), (2 * N, N // 2), (2 * N + N // 2, N // 2)]
+        for i, (c0, width) in enumerate(pieces):
             avg = psum_t.tile([P, N], F32, tag="xt")
             nc.tensor.matmul(
-                out=avg[:], lhsT=factor[:, 0:1].to_broadcast([P, P]), rhs=e_sb[:, b, :],
-                start=True, stop=True,
+                out=avg[:, 0:width], lhsT=factor[:, 0:1].to_broadcast([P, P]),
+                rhs=e_flat[:, c0 : c0 + width], start=True, stop=True,
             )
-            copy = nc.vector.tensor_copy if b % 2 == 0 else nc.scalar.copy
-            copy(out=avg_sb[0:1, b, :], in_=avg[0:1, :])
-        nc.sync.dma_start(
-            out=out_1.rearrange("(o n) -> o n", o=1),
-            in_=avg_sb[0:1].rearrange("o b n -> o (b n)"),
-        )
+            copy = nc.vector.tensor_copy if i % 2 == 0 else nc.scalar.copy
+            copy(out=avg_sb[0:1, c0 : c0 + width], in_=avg[0:1, 0:width])
+        nc.sync.dma_start(out=out_1.rearrange("(o n) -> o n", o=1), in_=avg_sb[0:1, :])

@@ -25,6 +25,10 @@ QUAD = 4
 PAIR = 2
 QUADRANTS = 4
 SCALE_DMAS_PER_LOAD = 3
+QUADS_AHEAD = 2
+QUADS_PER_SLOT = 2
+SYNC_SCALE_SLOTS = (5, 6, 7, 8)
+FIRST_SLOT_WITH_SCALES_BEHIND = 2
 FILLERS = 6
 
 FLOPS = 2 * P * ALL_PASSES * K_PASS * N
@@ -77,24 +81,20 @@ def tile_gep_pa_kernel(
                 )
 
         all_jobs = [(s, q) for s in range(len(slots)) for q in range(QUADRANTS)]
-        load_scales(nc.gpsimd, F32, [(s, q) for s, q in all_jobs if slots[s][0] == 2])
-        scale_jobs = [(s, q) for s, q in all_jobs if slots[s][0] < 2]
+        load_scales(nc.gpsimd, F32, [(s, q) for s, q in all_jobs if s not in SYNC_SCALE_SLOTS])
+        scale_jobs = [(s, q) for s, q in all_jobs if s in SYNC_SCALE_SLOTS]
 
-        loads = 0
+        issued = 0
         x_sb = []
-        for c in range(ALL_PASSES // X_CHUNK):
-            x_c = keep.tile([P, X_CHUNK * K_PASS], BF16, name="x%d" % c)
-            nc.sync.dma_start(
-                out=x_c[:], in_=target_grad[:, c * X_CHUNK * K_PASS : (c + 1) * X_CHUNK * K_PASS]
-            )
-            x_sb.append(x_c)
-            load_scales(
-                nc.sync, I32,
-                scale_jobs[loads * SCALE_DMAS_PER_LOAD : (loads + 1) * SCALE_DMAS_PER_LOAD],
-            )
-            loads += 1
         w_sb = []
         for s in range(len(slots)):
+            if s < ALL_PASSES // X_CHUNK:
+                x_c = keep.tile([P, X_CHUNK * K_PASS], BF16, name="x%d" % s)
+                nc.scalar.dma_start(
+                    out=x_c[:],
+                    in_=target_grad[:, s * X_CHUNK * K_PASS : (s + 1) * X_CHUNK * K_PASS],
+                )
+                x_sb.append(x_c)
             b, g0, n = slots[s]
             w_s = keep.tile([P, n, N], U32, name="w%d" % s, align_bytes=64)
             nc.sync.dma_start(
@@ -102,12 +102,10 @@ def tile_gep_pa_kernel(
                 in_=words[b][g0 : g0 + n].rearrange("g p n t -> p g (n t)").bitcast(I32),
             )
             w_sb.append(w_s)
-            load_scales(
-                nc.sync, I32,
-                scale_jobs[loads * SCALE_DMAS_PER_LOAD : (loads + 1) * SCALE_DMAS_PER_LOAD],
-            )
-            loads += 1
-        assert loads * SCALE_DMAS_PER_LOAD >= len(scale_jobs)
+            if s >= FIRST_SLOT_WITH_SCALES_BEHIND:
+                load_scales(nc.sync, I32, scale_jobs[issued : issued + SCALE_DMAS_PER_LOAD])
+                issued += SCALE_DMAS_PER_LOAD
+        assert issued >= len(scale_jobs)
 
         x_codes = keep.tile([P, ALL_PASSES * P], U32, align_bytes=64)
         x_planes = keep.tile([P, ALL_PASSES * P], U8, align_bytes=64)
@@ -118,8 +116,7 @@ def tile_gep_pa_kernel(
                 out=x_codes[:, cols].bitcast(FP8X4), scales=x_planes[:, cols], in_=grouped[:]
             )
 
-        waiting = None
-        for g0 in range(0, ALL_PASSES, QUAD):
+        def transpose_quad(g0):
             grouped = stage.tile([P, QUAD * P * PACK], BF16, align_bytes=64)
             grouped_words = grouped[:].bitcast(F32).rearrange(
                 "p (g b u) -> p g b u", g=QUAD, b=P
@@ -139,10 +136,23 @@ def tile_gep_pa_kernel(
                     out=grouped_words[:, h * PAIR : (h + 1) * PAIR],
                     in_=xt[:].rearrange("p g u b -> p g b u"),
                 )
-            if waiting is not None:
-                quantise(*waiting)
-            waiting = (g0, grouped)
-        quantise(*waiting)
+            return grouped
+
+        waiting = []
+
+        def quantise_waiting():
+            for first_pass, grouped in waiting:
+                quantise(first_pass, grouped)
+            waiting.clear()
+
+        def next_quad(g0):
+            grouped = transpose_quad(g0)
+            quantise_waiting()
+            waiting.append((g0, grouped))
+
+        for g0 in range(0, QUADS_AHEAD * QUAD, QUAD):
+            next_quad(g0)
+        later_quads = list(range(QUADS_AHEAD * QUAD, ALL_PASSES, QUAD))
 
         e_sb = keep.tile([P, 3, N], F32)
         squares = keep.tile([P, 3, N], F32)
@@ -158,6 +168,8 @@ def tile_gep_pa_kernel(
             accs.append(acc)
         for s in range(len(slots)):
             b, g0, n = slots[s]
+            if s == 0 or not later_quads:
+                quantise_waiting()
             for i in range(n):
                 g = FIRST_PASS[b] + g0 + i
                 nc.tensor.matmul_mx(
@@ -176,6 +188,9 @@ def tile_gep_pa_kernel(
                 )
                 if b < 2:
                     keep_embedding(b, accs[b])
+            for first_pass in later_quads[0:QUADS_PER_SLOT]:
+                next_quad(first_pass)
+                later_quads.remove(first_pass)
 
         filler = psum_d.tile([P, P], F32)
         for i in range(FILLERS):

from contextlib import ExitStack

import concourse.mybir as mybir
from concourse.masks import make_identity

F32 = mybir.dt.float32
BF16 = mybir.dt.bfloat16
I32 = mybir.dt.int32
U32 = mybir.dt.uint32
U8 = mybir.dt.uint8
FP8X4 = mybir.dt.float8_e4m3fn_x4
ACT = mybir.ActivationFunctionType
ALU = mybir.AluOpType

P = 128
PACK = 4
K_PASS = P * PACK
N = 512
PASSES = (8, 18, 14)
FIRST_PASS = (0, 8, 26)
ALL_PASSES = 40

X_CHUNK = 8
QUAD = 4
PAIR = 2
QUADRANTS = 4
SCALE_DMAS_PER_LOAD = 3
QUADS_AHEAD = 2
QUADS_PER_SLOT = 2
SYNC_SCALE_SLOTS = (5, 6, 7, 8)
FIRST_SLOT_WITH_SCALES_BEHIND = 2
FILLERS = 6

FLOPS = 2 * P * ALL_PASSES * K_PASS * N


def tile_gep_pa_kernel(
    tc,
    target_grad,
    bases0_words,
    bases0_scales,
    bases1_words,
    bases1_scales,
    bases2_words,
    bases2_scales,
    out_0,
    out_1,
):
    nc = tc.nc
    words = (bases0_words, bases1_words, bases2_words)
    scales = (bases0_scales, bases1_scales, bases2_scales)

    with ExitStack() as ctx:
        ctx.enter_context(tc.manual_schedule())
        keep = ctx.enter_context(tc.tile_pool(name="keep", bufs=1))
        stage = ctx.enter_context(tc.tile_pool(name="stage", bufs=3))
        psum_t = ctx.enter_context(tc.psum_pool(name="psum_t", bufs=4))
        psum_e = ctx.enter_context(tc.psum_pool(name="psum_e", bufs=1))
        psum_d = ctx.enter_context(tc.psum_pool(name="psum_d", bufs=1))

        slots = []
        for b in range(3):
            for g0 in range(0, PASSES[b], QUAD):
                slots.append((b, g0, min(QUAD, PASSES[b] - g0)))

        planes = keep.tile([P, len(slots) * N], U8, align_bytes=64)
        nc.vector.memset(planes[:].bitcast(I32), 0)
        one = keep.tile([P, 1], F32)
        nc.vector.memset(one[:], 1.0)
        warm = keep.tile([P, 1], F32)
        nc.scalar.activation(out=warm[:], in_=one[:], func=ACT.Abs_reciprocal_sqrt)
        ident = keep.tile([P, P], F32)
        make_identity(nc, ident[:])

        def load_scales(queue, view, jobs):
            for s, q in jobs:
                b, g0, n = slots[s]
                queue.dma_start(
                    out=planes[32 * q : 32 * q + 4 * n, s * N : (s + 1) * N].bitcast(view),
                    in_=scales[b][g0 : g0 + n, 4 * q : 4 * q + 4, :].bitcast(view),
                )

        all_jobs = [(s, q) for s in range(len(slots)) for q in range(QUADRANTS)]
        load_scales(nc.gpsimd, F32, [(s, q) for s, q in all_jobs if s not in SYNC_SCALE_SLOTS])
        scale_jobs = [(s, q) for s, q in all_jobs if s in SYNC_SCALE_SLOTS]

        issued = 0
        x_sb = []
        w_sb = []
        for s in range(len(slots)):
            if s < ALL_PASSES // X_CHUNK:
                x_c = keep.tile([P, X_CHUNK * K_PASS], BF16, name="x%d" % s)
                nc.scalar.dma_start(
                    out=x_c[:],
                    in_=target_grad[:, s * X_CHUNK * K_PASS : (s + 1) * X_CHUNK * K_PASS],
                )
                x_sb.append(x_c)
            b, g0, n = slots[s]
            w_s = keep.tile([P, n, N], U32, name="w%d" % s, align_bytes=64)
            nc.sync.dma_start(
                out=w_s[:].bitcast(I32),
                in_=words[b][g0 : g0 + n].rearrange("g p n t -> p g (n t)").bitcast(I32),
            )
            w_sb.append(w_s)
            if s >= FIRST_SLOT_WITH_SCALES_BEHIND:
                load_scales(nc.sync, I32, scale_jobs[issued : issued + SCALE_DMAS_PER_LOAD])
                issued += SCALE_DMAS_PER_LOAD
        assert issued >= len(scale_jobs)

        x_codes = keep.tile([P, ALL_PASSES * P], U32, align_bytes=64)
        x_planes = keep.tile([P, ALL_PASSES * P], U8, align_bytes=64)

        def quantise(first_pass, grouped):
            cols = slice(first_pass * P, (first_pass + QUAD) * P)
            nc.vector.quantize_mx(
                out=x_codes[:, cols].bitcast(FP8X4), scales=x_planes[:, cols], in_=grouped[:]
            )

        def transpose_quad(g0):
            grouped = stage.tile([P, QUAD * P * PACK], BF16, align_bytes=64)
            grouped_words = grouped[:].bitcast(F32).rearrange(
                "p (g b u) -> p g b u", g=QUAD, b=P
            )
            for h in range(QUAD // PAIR):
                xt = psum_t.tile([P, PAIR, 2, P], F32)
                for j in range(PAIR):
                    g = g0 + h * PAIR + j
                    x_words = x_sb[g // X_CHUNK][:].bitcast(F32)
                    w0 = (g % X_CHUNK) * (K_PASS // 2)
                    for u in range(2):
                        nc.tensor.transpose(
                            xt[:, j, u, :], x_words[:, w0 + u : w0 + K_PASS // 2 : 2], ident[:]
                        )
                copy = nc.vector.tensor_copy if h % 2 == 0 else nc.scalar.copy
                copy(
                    out=grouped_words[:, h * PAIR : (h + 1) * PAIR],
                    in_=xt[:].rearrange("p g u b -> p g b u"),
                )
            return grouped

        waiting = []

        def quantise_waiting():
            for first_pass, grouped in waiting:
                quantise(first_pass, grouped)
            waiting.clear()

        def next_quad(g0):
            grouped = transpose_quad(g0)
            quantise_waiting()
            waiting.append((g0, grouped))

        for g0 in range(0, QUADS_AHEAD * QUAD, QUAD):
            next_quad(g0)
        later_quads = list(range(QUADS_AHEAD * QUAD, ALL_PASSES, QUAD))

        e_sb = keep.tile([P, 3, N], F32)
        squares = keep.tile([P, 3, N], F32)
        sumsq = keep.tile([P, 3], F32)

        def keep_embedding(b, acc):
            nc.vector.tensor_copy(out=e_sb[:, b, :], in_=acc[:])
            nc.sync.dma_start(out=out_0[:, b * N : (b + 1) * N], in_=e_sb[:, b, :])

        accs = []
        for b in range(3):
            acc = psum_e.tile([P, N], F32, name="acc%d" % b)
            accs.append(acc)
        for s in range(len(slots)):
            b, g0, n = slots[s]
            if s == 0 or not later_quads:
                quantise_waiting()
            for i in range(n):
                g = FIRST_PASS[b] + g0 + i
                nc.tensor.matmul_mx(
                    out=accs[b][:],
                    lhsT=x_codes[:, g * P : (g + 1) * P].bitcast(FP8X4),
                    lhsT_scale=x_planes[:, g * P : (g + 1) * P],
                    rhs=w_sb[s][:, i, :].bitcast(FP8X4),
                    rhs_scale=planes[4 * i : P, s * N : (s + 1) * N],
                    start=(g0 + i == 0),
                    stop=(g0 + i == PASSES[b] - 1),
                )
            if g0 + n == PASSES[b]:
                nc.scalar.activation(
                    out=squares[:, b, :], in_=accs[b][:], func=ACT.Square,
                    accum_out=sumsq[:, b : b + 1],
                )
                if b < 2:
                    keep_embedding(b, accs[b])
            for first_pass in later_quads[0:QUADS_PER_SLOT]:
                next_quad(first_pass)
                later_quads.remove(first_pass)

        filler = psum_d.tile([P, P], F32)
        for i in range(FILLERS):
            nc.tensor.matmul(out=filler[:], lhsT=ident[:], rhs=ident[:], start=True, stop=True)

        early = keep.tile([P, 1], F32)
        nc.vector.tensor_add(out=early[:], in0=sumsq[:, 0:1], in1=sumsq[:, 1:2])
        inverse = keep.tile([P, 1], F32)
        nc.scalar.activation(
            out=inverse[:], in_=sumsq[:, 2:3], func=ACT.Abs_reciprocal_sqrt, bias=early[:]
        )
        factor = keep.tile([P, 1], F32)
        nc.vector.tensor_scalar(
            out=factor[:], in0=inverse[:], scalar1=1.0, scalar2=1.0 / P, op0=ALU.min, op1=ALU.mult
        )
        keep_embedding(2, accs[2])

        avg_sb = keep.tile([P, 3 * N], F32)
        e_flat = e_sb[:].rearrange("p b n -> p (b n)")
        pieces = [(0, N), (N, N), (2 * N, N // 2), (2 * N + N // 2, N // 2)]
        for i, (c0, width) in enumerate(pieces):
            avg = psum_t.tile([P, N], F32, tag="xt")
            nc.tensor.matmul(
                out=avg[:, 0:width], lhsT=factor[:, 0:1].to_broadcast([P, P]),
                rhs=e_flat[:, c0 : c0 + width], start=True, stop=True,
            )
            copy = nc.vector.tensor_copy if i % 2 == 0 else nc.scalar.copy
            copy(out=avg_sb[0:1, c0 : c0 + width], in_=avg[0:1, 0:width])
        nc.sync.dma_start(out=out_1.rearrange("(o n) -> o n", o=1), in_=avg_sb[0:1, :])
